import numpy as np
import ml_dtypes


def mxq(x, axis, fmt="e4m3"):
    dtype, down = {"e4m3": (ml_dtypes.float8_e4m3fn, 7), "e5m2": (ml_dtypes.float8_e5m2, 14)}[fmt]
    v = np.moveaxis(np.asarray(x, np.float32).astype(ml_dtypes.bfloat16).astype(np.float64), axis, -1)
    blocks = v.reshape(v.shape[:-1] + (-1, 32))
    amax = np.abs(blocks).max(-1, keepdims=True)
    byte = np.maximum(np.where(amax > 0, np.frexp(amax)[1] - 1 + 127, 0) - down, 1)
    scale = np.exp2(byte - 127.0)
    codes = (blocks / scale).astype(np.float32).astype(dtype).astype(np.float64)
    return np.moveaxis((codes * scale).reshape(v.shape), -1, axis)


WIDE = False


def mx_kscale(k):
    if not WIDE:
        return np.ones(k)
    levels = np.array([10, -10, 5, -5, 0])
    a = np.random.permutation(np.resize(levels, k // 512 * 4)).reshape(k // 512, 4)
    idx = np.arange(k)
    return np.exp2(a[idx // 512, idx % 128 // 32])


BF16 = ml_dtypes.bfloat16


def bf(x):
    return np.asarray(x, np.float32).astype(BF16)


def f64(x):
    return np.asarray(x).astype(np.float64)


B, IN, H, OUT = 2048, 512, 512, 256
NG = 4
G = NG * H
X = IN - 1
Y = IN - X
EPS = 1e-5


def sigmoid(v):
    return 1.0 / (1.0 + np.exp(-v))


def bn(z, g, b):
    m = z.mean(axis=0)
    v = ((z - m) ** 2).mean(axis=0)
    return (z - m) / np.sqrt(v + EPS) * g + b


def setup_inputs():
    s, t = mx_kscale(IN), mx_kscale(H)
    return {
        "x": bf(np.random.standard_normal((B, X)) * s[:X]),
        "y": bf(np.random.standard_normal((B, Y)) * 3.0 * s[X:]),
        "h_prev": bf(np.random.standard_normal((B, H)) * t),
        "c_prev": bf(np.random.standard_normal((B, H))),
        "Wx": bf(np.random.standard_normal((G, IN)) / np.sqrt(IN) / s),
        "Wh": bf(np.random.standard_normal((G, H)) / np.sqrt(H) / t),
        "gx": bf(1.0 + 0.2 * np.random.standard_normal(G)),
        "bx": bf(0.2 * np.random.standard_normal(G)),
        "gh": bf(1.0 + 0.2 * np.random.standard_normal(G)),
        "bh": bf(0.2 * np.random.standard_normal(G)),
    }


def reference(x, y, h_prev, c_prev, Wx, Wh, gx, bx, gh, bh):
    inp = np.concatenate([f64(x), f64(y)], axis=1)
    zx = mxq(inp, 1, "e4m3") @ mxq(f64(Wx), 1, "e4m3").T
    zh = mxq(f64(h_prev), 1, "e4m3") @ mxq(f64(Wh), 1, "e4m3").T
    gates = bn(zx, f64(gx), f64(bx)) + bn(zh, f64(gh), f64(bh))
    f, i, o, g = np.split(gates, NG, axis=1)
    c_new = sigmoid(f) * f64(c_prev) + sigmoid(i) * np.tanh(g)
    h_new = sigmoid(o) * np.tanh(c_new)
    return h_new, c_new

@@ -1,0 +1,367 @@
+from contextlib import ExitStack
+
+import concourse.mybir as mybir
+from concourse.masks import make_identity
+
+F32 = mybir.dt.float32
+BF16 = mybir.dt.bfloat16
+U32 = mybir.dt.uint32
+U8 = mybir.dt.uint8
+FP8X4 = mybir.dt.float8_e4m3fn_x4
+ACT = mybir.ActivationFunctionType
+ALU = mybir.AluOpType
+
+P = 128
+PACK = 4
+BATCH = 2048
+FEATURES = P * PACK
+HIDDEN = 512
+GATES = 4
+F_GATE, I_GATE, O_GATE, G_GATE = 0, 1, 2, 3
+EPS = 1e-5
+
+ROW_TILES = BATCH // P
+CHUNK = 512
+CHUNKS = BATCH // CHUNK
+TILES_PER_CHUNK = CHUNK // P
+HIDDEN_TILES = HIDDEN // P
+GATE_TILES = GATES * HIDDEN_TILES
+WORDS = FEATURES // 2
+X_WHOLE_BLOCKS = 496
+STATS_DIM = 6
+
+FLOPS = 2 * 2 * BATCH * GATES * HIDDEN * FEATURES
+
+GATE_ORDER = (G_GATE, I_GATE, F_GATE, O_GATE)
+
+ITEMS = GATE_TILES * CHUNKS
+LEAD = 2
+LAG_NORM_X = 1
+LAG_FUNCTION = 2
+LAG_FIRST_PRODUCT = 3
+LAG_SECOND_PRODUCT = 7
+LAG_STORE = 9
+
+
+def tile_cleanlstm_pa_kernel(tc, x, y, h_prev, c_prev, Wx, Wh, gx, bx, gh, bh, out_0, out_1):
+    nc = tc.nc
+    with ExitStack() as ctx:
+        ctx.enter_context(tc.manual_schedule())
+        const = ctx.enter_context(tc.tile_pool(name="const", bufs=1))
+        raw = ctx.enter_context(tc.tile_pool(name="raw", bufs=1))
+        keep = ctx.enter_context(tc.tile_pool(name="keep", bufs=1))
+        stage = ctx.enter_context(tc.tile_pool(name="stage", bufs=4))
+        small = ctx.enter_context(tc.tile_pool(name="small", bufs=5))
+        gates = ctx.enter_context(tc.tile_pool(name="gates", bufs=6))
+        rows_pool = ctx.enter_context(tc.tile_pool(name="rows", bufs=4))
+        psum = ctx.enter_context(tc.psum_pool(name="psum", bufs=8))
+
+        def chunk_cols(c):
+            return slice(c * CHUNK, (c + 1) * CHUNK)
+
+        def chunk_tiles(c):
+            return slice(c * TILES_PER_CHUNK, (c + 1) * TILES_PER_CHUNK)
+
+        x_sb = raw.tile([P, ROW_TILES * FEATURES], BF16)
+        x_rows = x_sb[:].rearrange("p (t k) -> p t k", t=ROW_TILES)
+        x_dram = x.rearrange("(p t) k -> p t k", t=ROW_TILES)
+        x_tail = raw.tile([P, ROW_TILES, 16], BF16)
+        y_sb = raw.tile([P, ROW_TILES], BF16)
+        h_sb = raw.tile([P, ROW_TILES * FEATURES], BF16)
+        h_rows = h_sb[:].rearrange("p (t k) -> p t k", t=ROW_TILES)
+        h_dram = h_prev.rearrange("(p t) k -> p t k", t=ROW_TILES)
+        c_sb = raw.tile([P, ROW_TILES, HIDDEN], BF16)
+        wx_sb = raw.tile([P, HIDDEN_TILES * GATES * FEATURES], BF16)
+        wh_sb = raw.tile([P, HIDDEN_TILES * GATES * FEATURES], BF16)
+        wx_rows = wx_sb[:].rearrange("p (j g k) -> p j g k", j=HIDDEN_TILES, g=GATES)
+        wh_rows = wh_sb[:].rearrange("p (j g k) -> p j g k", j=HIDDEN_TILES, g=GATES)
+        wx_dram = Wx.rearrange("(g j p) k -> p j g k", g=GATES, j=HIDDEN_TILES)
+        wh_dram = Wh.rearrange("(g j p) k -> p j g k", g=GATES, j=HIDDEN_TILES)
+
+        n_tail = FEATURES - 1 - X_WHOLE_BLOCKS
+        nc.scalar.dma_start(out=x_tail[:, :, 0:n_tail], in_=x_dram[:, :, X_WHOLE_BLOCKS : FEATURES - 1])
+        nc.scalar.dma_start(out=y_sb[:], in_=y.rearrange("(p t) o -> p (t o)", t=ROW_TILES))
+        par_rows = const.tile([P, P], BF16)
+        nc.vector.memset(par_rows[:], 0.0)
+        for q, vec in enumerate((gx, gh, bx, bh)):
+            nc.scalar.dma_start(
+                out=par_rows[q * GATE_TILES : (q + 1) * GATE_TILES, :], in_=vec.rearrange("(t p) -> t p", p=P)
+            )
+
+        for c in range(CHUNKS):
+            nc.sync.dma_start(
+                out=x_rows[:, chunk_tiles(c), 0:X_WHOLE_BLOCKS], in_=x_dram[:, chunk_tiles(c), 0:X_WHOLE_BLOCKS]
+            )
+        nc.sync.dma_start(out=wx_rows[:, 0], in_=wx_dram[:, 0])
+        for c in range(CHUNKS):
+            nc.sync.dma_start(out=h_rows[:, chunk_tiles(c), :], in_=h_dram[:, chunk_tiles(c), :])
+        nc.sync.dma_start(out=wh_rows[:, 0], in_=wh_dram[:, 0])
+        nc.sync.dma_start(out=wx_rows[:, 1], in_=wx_dram[:, 1])
+        nc.sync.dma_start(out=wh_rows[:, 1], in_=wh_dram[:, 1])
+        nc.sync.dma_start(out=c_sb[:], in_=c_prev.rearrange("(p t) k -> p t k", t=ROW_TILES))
+        for j in range(2, HIDDEN_TILES):
+            nc.sync.dma_start(out=wx_rows[:, j], in_=wx_dram[:, j])
+            nc.sync.dma_start(out=wh_rows[:, j], in_=wh_dram[:, j])
+
+        ident_f32 = const.tile([P, P], F32)
+        make_identity(nc, ident_f32[:])
+        ident_bf16 = const.tile([P, P], BF16)
+        make_identity(nc, ident_bf16[:])
+        minus_half = const.tile([P, 2], F32)
+        nc.gpsimd.memset(minus_half[:], -0.5)
+
+        nc.vector.tensor_copy(out=x_rows[:, :, X_WHOLE_BLOCKS : FEATURES - 1], in_=x_tail[:, :, 0:n_tail])
+        nc.vector.tensor_copy(out=x_rows[:, :, FEATURES - 1 : FEATURES], in_=y_sb[:].unsqueeze(2))
+
+        x_codes = keep.tile([P, BATCH], U32, align_bytes=64)
+        x_scales = keep.tile([P, BATCH], U8, align_bytes=64)
+        h_codes = keep.tile([P, BATCH], U32, align_bytes=64)
+        h_scales = keep.tile([P, BATCH], U8, align_bytes=64)
+        wx_codes = keep.tile([P, GATES * HIDDEN], U32, align_bytes=64)
+        wx_scales = keep.tile([P, GATES * HIDDEN], U8, align_bytes=64)
+        wh_codes = keep.tile([P, GATES * HIDDEN], U32, align_bytes=64)
+        wh_scales = keep.tile([P, GATES * HIDDEN], U8, align_bytes=64)
+
+        x_words = x_sb[:].bitcast(F32).rearrange("p (t w) -> p t w", w=WORDS)
+        h_words = h_sb[:].bitcast(F32).rearrange("p (t w) -> p t w", w=WORDS)
+        wx_words = wx_sb[:].bitcast(F32).rearrange("p (t w) -> p t w", w=WORDS)
+        wh_words = wh_sb[:].bitcast(F32).rearrange("p (t w) -> p t w", w=WORDS)
+
+        def new_grouped():
+            grouped = stage.tile([P, CHUNK * PACK], BF16, tag="grouped", align_bytes=64)
+            return grouped
+
+        def transpose_256_rows(words, c, a, grouped):
+            grouped_words = grouped[:].bitcast(F32).rearrange("p (a t r u) -> p a t r u", a=2, t=2, u=2)
+            bank = psum.tile([P, 2, 2, P], F32, tag="bank")
+            for t in range(2):
+                for u in range(2):
+                    nc.tensor.transpose(
+                        bank[:, t, u, :], words[:, c * TILES_PER_CHUNK + 2 * a + t, u * P : (u + 1) * P], ident_f32[:]
+                    )
+            nc.scalar.copy(out=grouped_words[:, a], in_=bank[:].rearrange("p t u r -> p t r u"))
+
+        def quantise(grouped, codes, scales, c):
+            nc.vector.quantize_mx(
+                out=codes[:, chunk_cols(c)].bitcast(FP8X4), scales=scales[:, chunk_cols(c)], in_=grouped[:]
+            )
+
+        def quantise_chunk(words, codes, scales, c):
+            grouped = new_grouped()
+            for a in range(2):
+                transpose_256_rows(words, c, a, grouped)
+            quantise(grouped, codes, scales, c)
+
+        operands = (
+            (wx_codes, wx_scales, x_codes, x_scales),
+            (wh_codes, wh_scales, h_codes, h_scales),
+        )
+        order = [(j, gate) for j in range(HIDDEN_TILES) for gate in GATE_ORDER]
+
+        def project(s, n, c):
+            j, gate = order[n]
+            w_codes, w_scales, a_codes, a_scales = operands[s]
+            w_cols = slice((j * GATES + gate) * P, (j * GATES + gate + 1) * P)
+            z = psum.tile([P, CHUNK], F32, tag="bank")
+            nc.tensor.matmul_mx(
+                out=z[:],
+                lhsT=w_codes[:, w_cols].bitcast(FP8X4),
+                lhsT_scale=w_scales[:, w_cols],
+                rhs=a_codes[:, chunk_cols(c)].bitcast(FP8X4),
+                rhs_scale=a_scales[:, chunk_cols(c)],
+                start=True,
+                stop=True,
+            )
+            return z
+
+        stats = {}
+        slopes = {}
+        shifts = {}
+        values = {}
+        zx_banks = {}
+
+        def chunk_statistics(s, n, c):
+            z = project(s, n, c)
+            nc.vector.bn_stats(out=stats[n][:, s, c, :], in_=z[:])
+
+        mean_vars = {}
+        rstds = {}
+
+        def begin_coefficients(n):
+            mean_var = small.tile([P, 2, 2], F32, tag="mean_var")
+            for s in range(2):
+                nc.vector.bn_aggr(out=mean_var[:, s, :], in_=stats[n][:, s, :, :].rearrange("p c k -> p (c k)"))
+            rstd = small.tile([P, 2], F32, tag="rstd")
+            nc.vector.tensor_scalar_add(out=rstd[:], in0=mean_var[:, :, 1], scalar1=EPS)
+            nc.gpsimd.tensor_tensor(out=rstd[:], in0=rstd[:], in1=minus_half[:], op=ALU.pow)
+            mean_vars[n] = mean_var
+            rstds[n] = rstd
+
+        def finish_coefficients(n):
+            j, gate = order[n]
+            t = gate * HIDDEN_TILES + j
+            slope = small.tile([P, 2], F32, tag="slope")
+            nc.vector.tensor_mul(out=slope[:], in0=rstds[n][:], in1=par[:, 0:2, t])
+            shift = small.tile([P, 2], F32, tag="shift")
+            nc.vector.tensor_mul(out=shift[:], in0=mean_vars[n][:, :, 0], in1=slope[:])
+            nc.vector.tensor_sub(out=shift[:], in0=par[:, 2:4, t], in1=shift[:])
+            slopes[n] = slope
+            shifts[n] = shift
+
+        def new_stats(n):
+            stats_n = small.tile([P, 2, CHUNKS, STATS_DIM], F32, tag="stats")
+            stats[n] = stats_n
+
+        for n in range(LEAD):
+            new_stats(n)
+        for c in range(CHUNKS):
+            quantise_chunk(x_words, x_codes, x_scales, c)
+        quantise_chunk(wx_words, wx_codes, wx_scales, 0)
+        for n in range(LEAD):
+            for c in range(CHUNKS):
+                chunk_statistics(0, n, c)
+        for c in range(CHUNKS):
+            quantise_chunk(h_words, h_codes, h_scales, c)
+        quantise_chunk(wh_words, wh_codes, wh_scales, 0)
+        par_bank = psum.tile([P, P], BF16, tag="bank")
+        nc.tensor.transpose(par_bank[:], par_rows[:], ident_bf16[:])
+        par = const.tile([P, 4, GATE_TILES], F32)
+        nc.vector.tensor_copy(out=par[:].rearrange("p q t -> p (q t)"), in_=par_bank[:, 0 : 4 * GATE_TILES])
+        for n in range(LEAD):
+            for c in range(CHUNKS):
+                chunk_statistics(1, n, c)
+            begin_coefficients(n)
+        for n in range(LEAD):
+            finish_coefficients(n)
+
+        cell_t = keep.tile([P, HIDDEN_TILES, BATCH], BF16)
+        half_tiles = ROW_TILES // 2
+        next_grouped = {}
+
+        def first_sweep(i):
+            n, c = divmod(i, CHUNKS)
+            if n < GATE_TILES:
+                if c == 0:
+                    new_stats(n)
+                for s in range(2):
+                    chunk_statistics(s, n, c)
+                if c == CHUNKS - 1:
+                    begin_coefficients(n)
+            if c == 0 and LEAD < n <= GATE_TILES:
+                finish_coefficients(n - 1)
+
+        def norm_h(i):
+            if i >= ITEMS:
+                return
+            n, c = divmod(i, CHUNKS)
+            if c == 0:
+                value = gates.tile([P, BATCH], F32, tag="gate")
+                values[n] = value
+            zh = project(1, n, c)
+            nc.scalar.activation(
+                out=values[n][:, chunk_cols(c)],
+                in_=zh[:],
+                func=ACT.Identity,
+                scale=slopes[n][:, 1:2],
+                bias=shifts[n][:, 1:2],
+            )
+            zx_banks[i] = project(0, n, c)
+
+        def norm_x(i):
+            if i < 0 or i >= ITEMS:
+                return
+            n, c = divmod(i, CHUNKS)
+            part = values[n][:, chunk_cols(c)]
+            nc.vector.scalar_tensor_tensor(
+                out=part, in0=zx_banks[i][:], scalar=slopes[n][:, 0:1], in1=part, op0=ALU.mult, op1=ALU.add
+            )
+
+        def gate_function(i):
+            if i < 0 or i >= ITEMS:
+                return
+            n, c = divmod(i, CHUNKS)
+            part = values[n][:, chunk_cols(c)]
+            func = ACT.Tanh if order[n][1] == G_GATE else ACT.Sigmoid
+            nc.scalar.activation(out=part, in_=part, func=func, bias=shifts[n][:, 0:1])
+
+        def products_engine(n):
+            return nc.vector if n + LEAD >= GATE_TILES else nc.gpsimd
+
+        def first_product(i):
+            if i < 0 or i >= ITEMS:
+                return
+            n, c = divmod(i, CHUNKS)
+            j, gate = order[n]
+            cols = chunk_cols(c)
+            mine = values[n][:, cols]
+            candidate = values[j * GATES][:, cols]
+            if gate == I_GATE:
+                products_engine(n).tensor_tensor(out=candidate, in0=mine, in1=candidate, op=ALU.mult)
+            if gate == F_GATE:
+                products_engine(n).tensor_tensor(out=mine, in0=mine, in1=cell_t[:, j, cols], op=ALU.mult)
+
+        def second_product(i):
+            if i < 0 or i >= ITEMS:
+                return
+            n, c = divmod(i, CHUNKS)
+            j, gate = order[n]
+            cols = chunk_cols(c)
+            mine = values[n][:, cols]
+            candidate = values[j * GATES][:, cols]
+            if gate == F_GATE:
+                products_engine(n).tensor_tensor(out=mine, in0=mine, in1=candidate, op=ALU.add)
+            if gate == O_GATE:
+                products_engine(n).tensor_tensor(out=mine, in0=mine, in1=candidate, op=ALU.mult)
+
+        def store(i):
+            if i < 0 or i >= ITEMS:
+                return
+            n, c = divmod(i, CHUNKS)
+            j, gate = order[n]
+            if gate != F_GATE and gate != O_GATE:
+                return
+            if gate == F_GATE:
+                nc.scalar.activation(
+                    out=values[j * GATES][:, chunk_cols(c)], in_=values[n][:, chunk_cols(c)], func=ACT.Tanh
+                )
+            out = out_1 if gate == F_GATE else out_0
+            bank = psum.tile([P, TILES_PER_CHUNK, P], F32, tag="bank")
+            for t in range(TILES_PER_CHUNK):
+                first = (c * TILES_PER_CHUNK + t) * P
+                nc.tensor.transpose(bank[:, t, :], values[n][:, first : first + P], ident_f32[:])
+            rows = rows_pool.tile([P, TILES_PER_CHUNK, P], F32, tag="rows")
+            nc.scalar.copy(out=rows[:], in_=bank[:])
+            out_rows = out.rearrange("(p t) k -> p t k", t=ROW_TILES)
+            nc.sync.dma_start(out=out_rows[:, chunk_tiles(c), j * P : (j + 1) * P], in_=rows[:])
+
+        def prepare(i):
+            if i >= ITEMS:
+                return
+            n, c = divmod(i, CHUNKS)
+            j, gate = order[n]
+            if gate == G_GATE and j + 1 < HIDDEN_TILES:
+                s, a = divmod(c, 2)
+                if a == 0:
+                    next_grouped[s] = new_grouped()
+                transpose_256_rows((wx_words, wh_words)[s], j + 1, a, next_grouped[s])
+            if gate == I_GATE and c == 0 and j + 1 < HIDDEN_TILES:
+                quantise(next_grouped[0], wx_codes, wx_scales, j + 1)
+                quantise(next_grouped[1], wh_codes, wh_scales, j + 1)
+            if gate == I_GATE and c < 2:
+                bank = psum.tile([P, half_tiles, P], BF16, tag="bank")
+                for t in range(half_tiles):
+                    nc.tensor.transpose(bank[:, t, :], c_sb[:, c * half_tiles + t, j * P : (j + 1) * P], ident_bf16[:])
+                nc.scalar.copy(
+                    out=cell_t[:, j, c * half_tiles * P : (c + 1) * half_tiles * P],
+                    in_=bank[:].rearrange("p t r -> p (t r)"),
+                )
+
+        for i in range(ITEMS + LAG_STORE):
+            norm_x(i - LAG_NORM_X)
+            first_sweep(i + LEAD * CHUNKS)
+            norm_h(i)
+            gate_function(i - LAG_FUNCTION)
+            first_product(i - LAG_FIRST_PRODUCT)
+            second_product(i - LAG_SECOND_PRODUCT)
+            store(i - LAG_STORE)
+            prepare(i)

@@ -36,11 +36,12 @@ GATE_ORDER = (G_GATE, I_GATE, F_GATE, O_GATE)
 
 ITEMS = GATE_TILES * CHUNKS
 LEAD = 2
-LAG_NORM_X = 1
-LAG_FUNCTION = 2
-LAG_FIRST_PRODUCT = 3
-LAG_SECOND_PRODUCT = 7
-LAG_STORE = 9
+LAG_NORM_X = 2
+LAG_FUNCTION = 4
+LAG_FIRST_PRODUCT = 6
+LAG_SECOND_PRODUCT = 10
+LAG_TANH = 12
+LAG_STORE = 16
 
 
 def tile_cleanlstm_pa_kernel(tc, x, y, h_prev, c_prev, Wx, Wh, gx, bx, gh, bh, out_0, out_1):
@@ -52,7 +53,7 @@ def tile_cleanlstm_pa_kernel(tc, x, y, h_prev, c_prev, Wx, Wh, gx, bx, gh, bh, o
         keep = ctx.enter_context(tc.tile_pool(name="keep", bufs=1))
         stage = ctx.enter_context(tc.tile_pool(name="stage", bufs=4))
         small = ctx.enter_context(tc.tile_pool(name="small", bufs=5))
-        gates = ctx.enter_context(tc.tile_pool(name="gates", bufs=6))
+        gates = ctx.enter_context(tc.tile_pool(name="gates", bufs=7))
         rows_pool = ctx.enter_context(tc.tile_pool(name="rows", bufs=4))
         psum = ctx.enter_context(tc.psum_pool(name="psum", bufs=8))
 
@@ -96,12 +97,12 @@ def tile_cleanlstm_pa_kernel(tc, x, y, h_prev, c_prev, Wx, Wh, gx, bx, gh, bh, o
         for c in range(CHUNKS):
             nc.sync.dma_start(out=h_rows[:, chunk_tiles(c), :], in_=h_dram[:, chunk_tiles(c), :])
         nc.sync.dma_start(out=wh_rows[:, 0], in_=wh_dram[:, 0])
-        nc.sync.dma_start(out=wx_rows[:, 1], in_=wx_dram[:, 1])
-        nc.sync.dma_start(out=wh_rows[:, 1], in_=wh_dram[:, 1])
-        nc.sync.dma_start(out=c_sb[:], in_=c_prev.rearrange("(p t) k -> p t k", t=ROW_TILES))
-        for j in range(2, HIDDEN_TILES):
+        for j in (1, 2):
             nc.sync.dma_start(out=wx_rows[:, j], in_=wx_dram[:, j])
             nc.sync.dma_start(out=wh_rows[:, j], in_=wh_dram[:, j])
+        nc.sync.dma_start(out=c_sb[:], in_=c_prev.rearrange("(p t) k -> p t k", t=ROW_TILES))
+        nc.sync.dma_start(out=wx_rows[:, 3], in_=wx_dram[:, 3])
+        nc.sync.dma_start(out=wh_rows[:, 3], in_=wh_dram[:, 3])
 
         ident_f32 = const.tile([P, P], F32)
         make_identity(nc, ident_f32[:])
@@ -178,33 +179,27 @@ def tile_cleanlstm_pa_kernel(tc, x, y, h_prev, c_prev, Wx, Wh, gx, bx, gh, bh, o
         slopes = {}
         shifts = {}
         values = {}
-        zx_banks = {}
 
         def chunk_statistics(s, n, c):
             z = project(s, n, c)
             nc.vector.bn_stats(out=stats[n][:, s, c, :], in_=z[:])
 
-        mean_vars = {}
-        rstds = {}
-
-        def begin_coefficients(n):
+        def coefficients(n):
+            j, gate = order[n]
+            t = gate * HIDDEN_TILES + j
             mean_var = small.tile([P, 2, 2], F32, tag="mean_var")
             for s in range(2):
                 nc.vector.bn_aggr(out=mean_var[:, s, :], in_=stats[n][:, s, :, :].rearrange("p c k -> p (c k)"))
             rstd = small.tile([P, 2], F32, tag="rstd")
-            nc.vector.tensor_scalar_add(out=rstd[:], in0=mean_var[:, :, 1], scalar1=EPS)
+            nc.gpsimd.tensor_scalar(
+                out=rstd[:], in0=mean_var[:, :, 1], scalar1=1.0, scalar2=EPS, op0=ALU.mult, op1=ALU.add
+            )
             nc.gpsimd.tensor_tensor(out=rstd[:], in0=rstd[:], in1=minus_half[:], op=ALU.pow)
-            mean_vars[n] = mean_var
-            rstds[n] = rstd
-
-        def finish_coefficients(n):
-            j, gate = order[n]
-            t = gate * HIDDEN_TILES + j
             slope = small.tile([P, 2], F32, tag="slope")
-            nc.vector.tensor_mul(out=slope[:], in0=rstds[n][:], in1=par[:, 0:2, t])
+            nc.gpsimd.tensor_tensor(out=slope[:], in0=rstd[:], in1=par[:, 0:2, t], op=ALU.mult)
             shift = small.tile([P, 2], F32, tag="shift")
-            nc.vector.tensor_mul(out=shift[:], in0=mean_vars[n][:, :, 0], in1=slope[:])
-            nc.vector.tensor_sub(out=shift[:], in0=par[:, 2:4, t], in1=shift[:])
+            nc.gpsimd.tensor_tensor(out=shift[:], in0=mean_var[:, :, 0], in1=slope[:], op=ALU.mult)
+            nc.gpsimd.tensor_tensor(out=shift[:], in0=par[:, 2:4, t], in1=shift[:], op=ALU.subtract)
             slopes[n] = slope
             shifts[n] = shift
 
@@ -230,25 +225,24 @@ def tile_cleanlstm_pa_kernel(tc, x, y, h_prev, c_prev, Wx, Wh, gx, bx, gh, bh, o
         for n in range(LEAD):
             for c in range(CHUNKS):
                 chunk_statistics(1, n, c)
-            begin_coefficients(n)
-        for n in range(LEAD):
-            finish_coefficients(n)
+            coefficients(n)
+        quantise_chunk(wx_words, wx_codes, wx_scales, 1)
+        quantise_chunk(wh_words, wh_codes, wh_scales, 1)
 
         cell_t = keep.tile([P, HIDDEN_TILES, BATCH], BF16)
         half_tiles = ROW_TILES // 2
         next_grouped = {}
 
         def first_sweep(i):
+            if i >= ITEMS:
+                return
             n, c = divmod(i, CHUNKS)
-            if n < GATE_TILES:
-                if c == 0:
-                    new_stats(n)
-                for s in range(2):
-                    chunk_statistics(s, n, c)
-                if c == CHUNKS - 1:
-                    begin_coefficients(n)
-            if c == 0 and LEAD < n <= GATE_TILES:
-                finish_coefficients(n - 1)
+            if c == 0:
+                new_stats(n)
+            for s in range(2):
+                chunk_statistics(s, n, c)
+            if c == CHUNKS - 1:
+                coefficients(n)
 
         def norm_h(i):
             if i >= ITEMS:
@@ -265,15 +259,15 @@ def tile_cleanlstm_pa_kernel(tc, x, y, h_prev, c_prev, Wx, Wh, gx, bx, gh, bh, o
                 scale=slopes[n][:, 1:2],
                 bias=shifts[n][:, 1:2],
             )
-            zx_banks[i] = project(0, n, c)
 
         def norm_x(i):
             if i < 0 or i >= ITEMS:
                 return
             n, c = divmod(i, CHUNKS)
             part = values[n][:, chunk_cols(c)]
+            zx = project(0, n, c)
             nc.vector.scalar_tensor_tensor(
-                out=part, in0=zx_banks[i][:], scalar=slopes[n][:, 0:1], in1=part, op0=ALU.mult, op1=ALU.add
+                out=part, in0=zx[:], scalar=slopes[n][:, 0:1], in1=part, op0=ALU.mult, op1=ALU.add
             )
 
         def gate_function(i):
@@ -284,8 +278,11 @@ def tile_cleanlstm_pa_kernel(tc, x, y, h_prev, c_prev, Wx, Wh, gx, bx, gh, bh, o
             func = ACT.Tanh if order[n][1] == G_GATE else ACT.Sigmoid
             nc.scalar.activation(out=part, in_=part, func=func, bias=shifts[n][:, 0:1])
 
+        def vector_is_free(n):
+            return n + LEAD >= GATE_TILES
+
         def products_engine(n):
-            return nc.vector if n + LEAD >= GATE_TILES else nc.gpsimd
+            return nc.vector if vector_is_free(n) else nc.gpsimd
 
         def first_product(i):
             if i < 0 or i >= ITEMS:
@@ -313,6 +310,16 @@ def tile_cleanlstm_pa_kernel(tc, x, y, h_prev, c_prev, Wx, Wh, gx, bx, gh, bh, o
             if gate == O_GATE:
                 products_engine(n).tensor_tensor(out=mine, in0=mine, in1=candidate, op=ALU.mult)
 
+        def cell_tanh(i):
+            if i < 0 or i >= ITEMS:
+                return
+            n, c = divmod(i, CHUNKS)
+            j, gate = order[n]
+            if gate == F_GATE:
+                nc.scalar.activation(
+                    out=values[j * GATES][:, chunk_cols(c)], in_=values[n][:, chunk_cols(c)], func=ACT.Tanh
+                )
+
         def store(i):
             if i < 0 or i >= ITEMS:
                 return
@@ -320,17 +327,16 @@ def tile_cleanlstm_pa_kernel(tc, x, y, h_prev, c_prev, Wx, Wh, gx, bx, gh, bh, o
             j, gate = order[n]
             if gate != F_GATE and gate != O_GATE:
                 return
-            if gate == F_GATE:
-                nc.scalar.activation(
-                    out=values[j * GATES][:, chunk_cols(c)], in_=values[n][:, chunk_cols(c)], func=ACT.Tanh
-                )
             out = out_1 if gate == F_GATE else out_0
             bank = psum.tile([P, TILES_PER_CHUNK, P], F32, tag="bank")
             for t in range(TILES_PER_CHUNK):
                 first = (c * TILES_PER_CHUNK + t) * P
                 nc.tensor.transpose(bank[:, t, :], values[n][:, first : first + P], ident_f32[:])
             rows = rows_pool.tile([P, TILES_PER_CHUNK, P], F32, tag="rows")
-            nc.scalar.copy(out=rows[:], in_=bank[:])
+            if vector_is_free(n):
+                nc.vector.tensor_copy(out=rows[:], in_=bank[:])
+            else:
+                nc.scalar.copy(out=rows[:], in_=bank[:])
             out_rows = out.rearrange("(p t) k -> p t k", t=ROW_TILES)
             nc.sync.dma_start(out=out_rows[:, chunk_tiles(c), j * P : (j + 1) * P], in_=rows[:])
 
@@ -339,20 +345,21 @@ def tile_cleanlstm_pa_kernel(tc, x, y, h_prev, c_prev, Wx, Wh, gx, bx, gh, bh, o
                 return
             n, c = divmod(i, CHUNKS)
             j, gate = order[n]
-            if gate == G_GATE and j + 1 < HIDDEN_TILES:
+            if gate == G_GATE and j + 2 < HIDDEN_TILES:
                 s, a = divmod(c, 2)
                 if a == 0:
                     next_grouped[s] = new_grouped()
-                transpose_256_rows((wx_words, wh_words)[s], j + 1, a, next_grouped[s])
-            if gate == I_GATE and c == 0 and j + 1 < HIDDEN_TILES:
-                quantise(next_grouped[0], wx_codes, wx_scales, j + 1)
-                quantise(next_grouped[1], wh_codes, wh_scales, j + 1)
-            if gate == I_GATE and c < 2:
+                transpose_256_rows((wx_words, wh_words)[s], j + 2, a, next_grouped[s])
+            if gate == I_GATE and c == 0 and j + 2 < HIDDEN_TILES:
+                quantise(next_grouped[0], wx_codes, wx_scales, j + 2)
+                quantise(next_grouped[1], wh_codes, wh_scales, j + 2)
+            if j == 0 and (gate == I_GATE or gate == F_GATE):
+                jc, a = divmod(i - CHUNKS, 2)
                 bank = psum.tile([P, half_tiles, P], BF16, tag="bank")
                 for t in range(half_tiles):
-                    nc.tensor.transpose(bank[:, t, :], c_sb[:, c * half_tiles + t, j * P : (j + 1) * P], ident_bf16[:])
+                    nc.tensor.transpose(bank[:, t, :], c_sb[:, a * half_tiles + t, jc * P : (jc + 1) * P], ident_bf16[:])
                 nc.scalar.copy(
-                    out=cell_t[:, j, c * half_tiles * P : (c + 1) * half_tiles * P],
+                    out=cell_t[:, jc, a * half_tiles * P : (a + 1) * half_tiles * P],
                     in_=bank[:].rearrange("p t r -> p (t r)"),
                 )
 
@@ -363,5 +370,6 @@ def tile_cleanlstm_pa_kernel(tc, x, y, h_prev, c_prev, Wx, Wh, gx, bx, gh, bh, o
             gate_function(i - LAG_FUNCTION)
             first_product(i - LAG_FIRST_PRODUCT)
             second_product(i - LAG_SECOND_PRODUCT)
+            cell_tanh(i - LAG_TANH)
             store(i - LAG_STORE)
             prepare(i)

@@ -35,7 +35,8 @@ FLOPS = 2 * 2 * BATCH * GATES * HIDDEN * FEATURES
 GATE_ORDER = (G_GATE, I_GATE, F_GATE, O_GATE)
 
 ITEMS = GATE_TILES * CHUNKS
-LEAD = 2
+LEAD = 6
+VECTOR_TILES = 2
 LAG_NORM_X = 2
 LAG_FUNCTION = 4
 LAG_FIRST_PRODUCT = 6
@@ -89,14 +90,14 @@ def tile_cleanlstm_pa_kernel(tc, x, y, h_prev, c_prev, Wx, Wh, gx, bx, gh, bh, o
                 out=par_rows[q * GATE_TILES : (q + 1) * GATE_TILES, :], in_=vec.rearrange("(t p) -> t p", p=P)
             )
 
+        nc.sync.dma_start(out=wx_rows[:, 0], in_=wx_dram[:, 0])
+        nc.sync.dma_start(out=wh_rows[:, 0], in_=wh_dram[:, 0])
         for c in range(CHUNKS):
             nc.sync.dma_start(
                 out=x_rows[:, chunk_tiles(c), 0:X_WHOLE_BLOCKS], in_=x_dram[:, chunk_tiles(c), 0:X_WHOLE_BLOCKS]
             )
-        nc.sync.dma_start(out=wx_rows[:, 0], in_=wx_dram[:, 0])
         for c in range(CHUNKS):
             nc.sync.dma_start(out=h_rows[:, chunk_tiles(c), :], in_=h_dram[:, chunk_tiles(c), :])
-        nc.sync.dma_start(out=wh_rows[:, 0], in_=wh_dram[:, 0])
         for j in (1, 2):
             nc.sync.dma_start(out=wx_rows[:, j], in_=wx_dram[:, j])
             nc.sync.dma_start(out=wh_rows[:, j], in_=wh_dram[:, j])
@@ -207,25 +208,26 @@ def tile_cleanlstm_pa_kernel(tc, x, y, h_prev, c_prev, Wx, Wh, gx, bx, gh, bh, o
             stats_n = small.tile([P, 2, CHUNKS, STATS_DIM], F32, tag="stats")
             stats[n] = stats_n
 
-        for n in range(LEAD):
-            new_stats(n)
-        for c in range(CHUNKS):
-            quantise_chunk(x_words, x_codes, x_scales, c)
         quantise_chunk(wx_words, wx_codes, wx_scales, 0)
-        for n in range(LEAD):
-            for c in range(CHUNKS):
-                chunk_statistics(0, n, c)
-        for c in range(CHUNKS):
-            quantise_chunk(h_words, h_codes, h_scales, c)
         quantise_chunk(wh_words, wh_codes, wh_scales, 0)
         par_bank = psum.tile([P, P], BF16, tag="bank")
         nc.tensor.transpose(par_bank[:], par_rows[:], ident_bf16[:])
         par = const.tile([P, 4, GATE_TILES], F32)
         nc.vector.tensor_copy(out=par[:].rearrange("p q t -> p (q t)"), in_=par_bank[:, 0 : 4 * GATE_TILES])
-        for n in range(LEAD):
-            for c in range(CHUNKS):
-                chunk_statistics(1, n, c)
-            coefficients(n)
+        head_items = [divmod(i, CHUNKS) for i in range(LEAD)]
+        for n, c in head_items:
+            if c == 0:
+                new_stats(n)
+        activations = ((x_words, x_codes, x_scales), (h_words, h_codes, h_scales))
+        for s, (words, codes, scales) in enumerate(activations):
+            for chunk in range(CHUNKS):
+                quantise_chunk(words, codes, scales, chunk)
+                for n, c in head_items:
+                    if c == chunk:
+                        chunk_statistics(s, n, c)
+        for n, c in head_items:
+            if c == CHUNKS - 1:
+                coefficients(n)
         quantise_chunk(wx_words, wx_codes, wx_scales, 1)
         quantise_chunk(wh_words, wh_codes, wh_scales, 1)
 
@@ -279,7 +281,7 @@ def tile_cleanlstm_pa_kernel(tc, x, y, h_prev, c_prev, Wx, Wh, gx, bx, gh, bh, o
             nc.scalar.activation(out=part, in_=part, func=func, bias=shifts[n][:, 0:1])
 
         def vector_is_free(n):
-            return n + LEAD >= GATE_TILES
+            return n + VECTOR_TILES >= GATE_TILES
 
         def products_engine(n):
             return nc.vector if vector_is_free(n) else nc.gpsimd
@@ -365,7 +367,7 @@ def tile_cleanlstm_pa_kernel(tc, x, y, h_prev, c_prev, Wx, Wh, gx, bx, gh, bh, o
 
         for i in range(ITEMS + LAG_STORE):
             norm_x(i - LAG_NORM_X)
-            first_sweep(i + LEAD * CHUNKS)
+            first_sweep(i + LEAD)
             norm_h(i)
             gate_function(i - LAG_FUNCTION)
             first_product(i - LAG_FIRST_PRODUCT)

@@ -36,6 +36,7 @@ GATE_ORDER = (G_GATE, I_GATE, F_GATE, O_GATE)
 
 ITEMS = GATE_TILES * CHUNKS
 LEAD = 6
+HEAD_LAG = 2
 VECTOR_TILES = 2
 LAG_NORM_X = 2
 LAG_FUNCTION = 4
@@ -43,6 +44,10 @@ LAG_FIRST_PRODUCT = 6
 LAG_SECOND_PRODUCT = 10
 LAG_TANH = 12
 LAG_STORE = 16
+SHORT_FIRST_PRODUCT = 5
+SHORT_SECOND_PRODUCT = 6
+SHORT_TANH = 7
+SHORT_STORE = 7
 
 
 def tile_cleanlstm_pa_kernel(tc, x, y, h_prev, c_prev, Wx, Wh, gx, bx, gh, bh, out_0, out_1):
@@ -98,12 +103,12 @@ def tile_cleanlstm_pa_kernel(tc, x, y, h_prev, c_prev, Wx, Wh, gx, bx, gh, bh, o
             )
         for c in range(CHUNKS):
             nc.sync.dma_start(out=h_rows[:, chunk_tiles(c), :], in_=h_dram[:, chunk_tiles(c), :])
-        for j in (1, 2):
+        nc.sync.dma_start(out=wx_rows[:, 1], in_=wx_dram[:, 1])
+        nc.sync.dma_start(out=wh_rows[:, 1], in_=wh_dram[:, 1])
+        nc.sync.dma_start(out=c_sb[:], in_=c_prev.rearrange("(p t) k -> p t k", t=ROW_TILES))
+        for j in range(2, HIDDEN_TILES):
             nc.sync.dma_start(out=wx_rows[:, j], in_=wx_dram[:, j])
             nc.sync.dma_start(out=wh_rows[:, j], in_=wh_dram[:, j])
-        nc.sync.dma_start(out=c_sb[:], in_=c_prev.rearrange("(p t) k -> p t k", t=ROW_TILES))
-        nc.sync.dma_start(out=wx_rows[:, 3], in_=wx_dram[:, 3])
-        nc.sync.dma_start(out=wh_rows[:, 3], in_=wh_dram[:, 3])
 
         ident_f32 = const.tile([P, P], F32)
         make_identity(nc, ident_f32[:])
@@ -219,17 +224,19 @@ def tile_cleanlstm_pa_kernel(tc, x, y, h_prev, c_prev, Wx, Wh, gx, bx, gh, bh, o
             if c == 0:
                 new_stats(n)
         activations = ((x_words, x_codes, x_scales), (h_words, h_codes, h_scales))
-        for s, (words, codes, scales) in enumerate(activations):
-            for chunk in range(CHUNKS):
-                quantise_chunk(words, codes, scales, chunk)
+        head_chunks = [(s, chunk) for s in range(2) for chunk in range(CHUNKS)]
+        for k in range(len(head_chunks) + HEAD_LAG):
+            if k < len(head_chunks):
+                s, chunk = head_chunks[k]
+                quantise_chunk(*activations[s], chunk)
+            if k >= HEAD_LAG:
+                s, chunk = head_chunks[k - HEAD_LAG]
                 for n, c in head_items:
                     if c == chunk:
                         chunk_statistics(s, n, c)
         for n, c in head_items:
             if c == CHUNKS - 1:
                 coefficients(n)
-        quantise_chunk(wx_words, wx_codes, wx_scales, 1)
-        quantise_chunk(wh_words, wh_codes, wh_scales, 1)
 
         cell_t = keep.tile([P, HIDDEN_TILES, BATCH], BF16)
         half_tiles = ROW_TILES // 2
@@ -283,12 +290,17 @@ def tile_cleanlstm_pa_kernel(tc, x, y, h_prev, c_prev, Wx, Wh, gx, bx, gh, bh, o
         def vector_is_free(n):
             return n + VECTOR_TILES >= GATE_TILES
 
+        def due(i, lag, short_lag):
+            items = []
+            for item, on_vector in ((i - lag, False), (i - short_lag, True)):
+                if 0 <= item < ITEMS and vector_is_free(item // CHUNKS) == on_vector:
+                    items.append(item)
+            return items
+
         def products_engine(n):
             return nc.vector if vector_is_free(n) else nc.gpsimd
 
         def first_product(i):
-            if i < 0 or i >= ITEMS:
-                return
             n, c = divmod(i, CHUNKS)
             j, gate = order[n]
             cols = chunk_cols(c)
@@ -300,8 +312,6 @@ def tile_cleanlstm_pa_kernel(tc, x, y, h_prev, c_prev, Wx, Wh, gx, bx, gh, bh, o
                 products_engine(n).tensor_tensor(out=mine, in0=mine, in1=cell_t[:, j, cols], op=ALU.mult)
 
         def second_product(i):
-            if i < 0 or i >= ITEMS:
-                return
             n, c = divmod(i, CHUNKS)
             j, gate = order[n]
             cols = chunk_cols(c)
@@ -313,8 +323,6 @@ def tile_cleanlstm_pa_kernel(tc, x, y, h_prev, c_prev, Wx, Wh, gx, bx, gh, bh, o
                 products_engine(n).tensor_tensor(out=mine, in0=mine, in1=candidate, op=ALU.mult)
 
         def cell_tanh(i):
-            if i < 0 or i >= ITEMS:
-                return
             n, c = divmod(i, CHUNKS)
             j, gate = order[n]
             if gate == F_GATE:
@@ -323,8 +331,6 @@ def tile_cleanlstm_pa_kernel(tc, x, y, h_prev, c_prev, Wx, Wh, gx, bx, gh, bh, o
                 )
 
         def store(i):
-            if i < 0 or i >= ITEMS:
-                return
             n, c = divmod(i, CHUNKS)
             j, gate = order[n]
             if gate != F_GATE and gate != O_GATE:
@@ -347,14 +353,14 @@ def tile_cleanlstm_pa_kernel(tc, x, y, h_prev, c_prev, Wx, Wh, gx, bx, gh, bh, o
                 return
             n, c = divmod(i, CHUNKS)
             j, gate = order[n]
-            if gate == G_GATE and j + 2 < HIDDEN_TILES:
+            if gate == G_GATE and j + 1 < HIDDEN_TILES:
                 s, a = divmod(c, 2)
                 if a == 0:
                     next_grouped[s] = new_grouped()
-                transpose_256_rows((wx_words, wh_words)[s], j + 2, a, next_grouped[s])
-            if gate == I_GATE and c == 0 and j + 2 < HIDDEN_TILES:
-                quantise(next_grouped[0], wx_codes, wx_scales, j + 2)
-                quantise(next_grouped[1], wh_codes, wh_scales, j + 2)
+                transpose_256_rows((wx_words, wh_words)[s], j + 1, a, next_grouped[s])
+            if gate == I_GATE and c == 0 and j + 1 < HIDDEN_TILES:
+                quantise(next_grouped[0], wx_codes, wx_scales, j + 1)
+                quantise(next_grouped[1], wh_codes, wh_scales, j + 1)
             if j == 0 and (gate == I_GATE or gate == F_GATE):
                 jc, a = divmod(i - CHUNKS, 2)
                 bank = psum.tile([P, half_tiles, P], BF16, tag="bank")
@@ -366,12 +372,21 @@ def tile_cleanlstm_pa_kernel(tc, x, y, h_prev, c_prev, Wx, Wh, gx, bx, gh, bh, o
                 )
 
         for i in range(ITEMS + LAG_STORE):
+            if i % 2 == 1:
+                for item in due(i, LAG_STORE, SHORT_STORE):
+                    store(item)
+                prepare(i)
             norm_x(i - LAG_NORM_X)
             first_sweep(i + LEAD)
             norm_h(i)
             gate_function(i - LAG_FUNCTION)
-            first_product(i - LAG_FIRST_PRODUCT)
-            second_product(i - LAG_SECOND_PRODUCT)
-            cell_tanh(i - LAG_TANH)
-            store(i - LAG_STORE)
-            prepare(i)
+            for item in due(i, LAG_FIRST_PRODUCT, SHORT_FIRST_PRODUCT):
+                first_product(item)
+            for item in due(i, LAG_SECOND_PRODUCT, SHORT_SECOND_PRODUCT):
+                second_product(item)
+            for item in due(i, LAG_TANH, SHORT_TANH):
+                cell_tanh(item)
+            if i % 2 == 0:
+                for item in due(i, LAG_STORE, SHORT_STORE):
+                    store(item)
+                prepare(i)

from contextlib import ExitStack

import concourse.mybir as mybir
from concourse.masks import make_identity

F32 = mybir.dt.float32
BF16 = mybir.dt.bfloat16
U32 = mybir.dt.uint32
U8 = mybir.dt.uint8
FP8X4 = mybir.dt.float8_e4m3fn_x4
ACT = mybir.ActivationFunctionType
ALU = mybir.AluOpType

P = 128
PACK = 4
BATCH = 2048
FEATURES = P * PACK
HIDDEN = 512
GATES = 4
F_GATE, I_GATE, O_GATE, G_GATE = 0, 1, 2, 3
EPS = 1e-5

ROW_TILES = BATCH // P
CHUNK = 512
CHUNKS = BATCH // CHUNK
TILES_PER_CHUNK = CHUNK // P
HIDDEN_TILES = HIDDEN // P
GATE_TILES = GATES * HIDDEN_TILES
WORDS = FEATURES // 2
X_WHOLE_BLOCKS = 496
STATS_DIM = 6

FLOPS = 2 * 2 * BATCH * GATES * HIDDEN * FEATURES

GATE_ORDER = (G_GATE, I_GATE, F_GATE, O_GATE)

ITEMS = GATE_TILES * CHUNKS
LEAD = 6
HEAD_LAG = 2
VECTOR_TILES = 2
LAG_NORM_X = 2
LAG_FUNCTION = 4
LAG_FIRST_PRODUCT = 6
LAG_SECOND_PRODUCT = 10
LAG_TANH = 12
LAG_STORE = 16
SHORT_FIRST_PRODUCT = 5
SHORT_SECOND_PRODUCT = 6
SHORT_TANH = 7
SHORT_STORE = 7


def tile_cleanlstm_pa_kernel(tc, x, y, h_prev, c_prev, Wx, Wh, gx, bx, gh, bh, out_0, out_1):
    nc = tc.nc
    with ExitStack() as ctx:
        ctx.enter_context(tc.manual_schedule())
        const = ctx.enter_context(tc.tile_pool(name="const", bufs=1))
        raw = ctx.enter_context(tc.tile_pool(name="raw", bufs=1))
        keep = ctx.enter_context(tc.tile_pool(name="keep", bufs=1))
        stage = ctx.enter_context(tc.tile_pool(name="stage", bufs=4))
        small = ctx.enter_context(tc.tile_pool(name="small", bufs=5))
        gates = ctx.enter_context(tc.tile_pool(name="gates", bufs=7))
        rows_pool = ctx.enter_context(tc.tile_pool(name="rows", bufs=4))
        psum = ctx.enter_context(tc.psum_pool(name="psum", bufs=8))

        def chunk_cols(c):
            return slice(c * CHUNK, (c + 1) * CHUNK)

        def chunk_tiles(c):
            return slice(c * TILES_PER_CHUNK, (c + 1) * TILES_PER_CHUNK)

        x_sb = raw.tile([P, ROW_TILES * FEATURES], BF16)
        x_rows = x_sb[:].rearrange("p (t k) -> p t k", t=ROW_TILES)
        x_dram = x.rearrange("(p t) k -> p t k", t=ROW_TILES)
        x_tail = raw.tile([P, ROW_TILES, 16], BF16)
        y_sb = raw.tile([P, ROW_TILES], BF16)
        h_sb = raw.tile([P, ROW_TILES * FEATURES], BF16)
        h_rows = h_sb[:].rearrange("p (t k) -> p t k", t=ROW_TILES)
        h_dram = h_prev.rearrange("(p t) k -> p t k", t=ROW_TILES)
        c_sb = raw.tile([P, ROW_TILES, HIDDEN], BF16)
        wx_sb = raw.tile([P, HIDDEN_TILES * GATES * FEATURES], BF16)
        wh_sb = raw.tile([P, HIDDEN_TILES * GATES * FEATURES], BF16)
        wx_rows = wx_sb[:].rearrange("p (j g k) -> p j g k", j=HIDDEN_TILES, g=GATES)
        wh_rows = wh_sb[:].rearrange("p (j g k) -> p j g k", j=HIDDEN_TILES, g=GATES)
        wx_dram = Wx.rearrange("(g j p) k -> p j g k", g=GATES, j=HIDDEN_TILES)
        wh_dram = Wh.rearrange("(g j p) k -> p j g k", g=GATES, j=HIDDEN_TILES)

        n_tail = FEATURES - 1 - X_WHOLE_BLOCKS
        nc.scalar.dma_start(out=x_tail[:, :, 0:n_tail], in_=x_dram[:, :, X_WHOLE_BLOCKS : FEATURES - 1])
        nc.scalar.dma_start(out=y_sb[:], in_=y.rearrange("(p t) o -> p (t o)", t=ROW_TILES))
        par_rows = const.tile([P, P], BF16)
        nc.vector.memset(par_rows[:], 0.0)
        for q, vec in enumerate((gx, gh, bx, bh)):
            nc.scalar.dma_start(
                out=par_rows[q * GATE_TILES : (q + 1) * GATE_TILES, :], in_=vec.rearrange("(t p) -> t p", p=P)
            )

        nc.sync.dma_start(out=wx_rows[:, 0], in_=wx_dram[:, 0])
        nc.sync.dma_start(out=wh_rows[:, 0], in_=wh_dram[:, 0])
        for c in range(CHUNKS):
            nc.sync.dma_start(
                out=x_rows[:, chunk_tiles(c), 0:X_WHOLE_BLOCKS], in_=x_dram[:, chunk_tiles(c), 0:X_WHOLE_BLOCKS]
            )
        for c in range(CHUNKS):
            nc.sync.dma_start(out=h_rows[:, chunk_tiles(c), :], in_=h_dram[:, chunk_tiles(c), :])
        nc.sync.dma_start(out=wx_rows[:, 1], in_=wx_dram[:, 1])
        nc.sync.dma_start(out=wh_rows[:, 1], in_=wh_dram[:, 1])
        nc.sync.dma_start(out=c_sb[:], in_=c_prev.rearrange("(p t) k -> p t k", t=ROW_TILES))
        for j in range(2, HIDDEN_TILES):
            nc.sync.dma_start(out=wx_rows[:, j], in_=wx_dram[:, j])
            nc.sync.dma_start(out=wh_rows[:, j], in_=wh_dram[:, j])

        ident_f32 = const.tile([P, P], F32)
        make_identity(nc, ident_f32[:])
        ident_bf16 = const.tile([P, P], BF16)
        make_identity(nc, ident_bf16[:])
        minus_half = const.tile([P, 2], F32)
        nc.gpsimd.memset(minus_half[:], -0.5)

        nc.vector.tensor_copy(out=x_rows[:, :, X_WHOLE_BLOCKS : FEATURES - 1], in_=x_tail[:, :, 0:n_tail])
        nc.vector.tensor_copy(out=x_rows[:, :, FEATURES - 1 : FEATURES], in_=y_sb[:].unsqueeze(2))

        x_codes = keep.tile([P, BATCH], U32, align_bytes=64)
        x_scales = keep.tile([P, BATCH], U8, align_bytes=64)
        h_codes = keep.tile([P, BATCH], U32, align_bytes=64)
        h_scales = keep.tile([P, BATCH], U8, align_bytes=64)
        wx_codes = keep.tile([P, GATES * HIDDEN], U32, align_bytes=64)
        wx_scales = keep.tile([P, GATES * HIDDEN], U8, align_bytes=64)
        wh_codes = keep.tile([P, GATES * HIDDEN], U32, align_bytes=64)
        wh_scales = keep.tile([P, GATES * HIDDEN], U8, align_bytes=64)

        x_words = x_sb[:].bitcast(F32).rearrange("p (t w) -> p t w", w=WORDS)
        h_words = h_sb[:].bitcast(F32).rearrange("p (t w) -> p t w", w=WORDS)
        wx_words = wx_sb[:].bitcast(F32).rearrange("p (t w) -> p t w", w=WORDS)
        wh_words = wh_sb[:].bitcast(F32).rearrange("p (t w) -> p t w", w=WORDS)

        def new_grouped():
            grouped = stage.tile([P, CHUNK * PACK], BF16, tag="grouped", align_bytes=64)
            return grouped

        def transpose_256_rows(words, c, a, grouped):
            grouped_words = grouped[:].bitcast(F32).rearrange("p (a t r u) -> p a t r u", a=2, t=2, u=2)
            bank = psum.tile([P, 2, 2, P], F32, tag="bank")
            for t in range(2):
                for u in range(2):
                    nc.tensor.transpose(
                        bank[:, t, u, :], words[:, c * TILES_PER_CHUNK + 2 * a + t, u * P : (u + 1) * P], ident_f32[:]
                    )
            nc.scalar.copy(out=grouped_words[:, a], in_=bank[:].rearrange("p t u r -> p t r u"))

        def quantise(grouped, codes, scales, c):
            nc.vector.quantize_mx(
                out=codes[:, chunk_cols(c)].bitcast(FP8X4), scales=scales[:, chunk_cols(c)], in_=grouped[:]
            )

        def quantise_chunk(words, codes, scales, c):
            grouped = new_grouped()
            for a in range(2):
                transpose_256_rows(words, c, a, grouped)
            quantise(grouped, codes, scales, c)

        operands = (
            (wx_codes, wx_scales, x_codes, x_scales),
            (wh_codes, wh_scales, h_codes, h_scales),
        )
        order = [(j, gate) for j in range(HIDDEN_TILES) for gate in GATE_ORDER]

        def project(s, n, c):
            j, gate = order[n]
            w_codes, w_scales, a_codes, a_scales = operands[s]
            w_cols = slice((j * GATES + gate) * P, (j * GATES + gate + 1) * P)
            z = psum.tile([P, CHUNK], F32, tag="bank")
            nc.tensor.matmul_mx(
                out=z[:],
                lhsT=w_codes[:, w_cols].bitcast(FP8X4),
                lhsT_scale=w_scales[:, w_cols],
                rhs=a_codes[:, chunk_cols(c)].bitcast(FP8X4),
                rhs_scale=a_scales[:, chunk_cols(c)],
                start=True,
                stop=True,
            )
            return z

        stats = {}
        slopes = {}
        shifts = {}
        values = {}

        def chunk_statistics(s, n, c):
            z = project(s, n, c)
            nc.vector.bn_stats(out=stats[n][:, s, c, :], in_=z[:])

        def coefficients(n):
            j, gate = order[n]
            t = gate * HIDDEN_TILES + j
            mean_var = small.tile([P, 2, 2], F32, tag="mean_var")
            for s in range(2):
                nc.vector.bn_aggr(out=mean_var[:, s, :], in_=stats[n][:, s, :, :].rearrange("p c k -> p (c k)"))
            rstd = small.tile([P, 2], F32, tag="rstd")
            nc.gpsimd.tensor_scalar(
                out=rstd[:], in0=mean_var[:, :, 1], scalar1=1.0, scalar2=EPS, op0=ALU.mult, op1=ALU.add
            )
            nc.gpsimd.tensor_tensor(out=rstd[:], in0=rstd[:], in1=minus_half[:], op=ALU.pow)
            slope = small.tile([P, 2], F32, tag="slope")
            nc.gpsimd.tensor_tensor(out=slope[:], in0=rstd[:], in1=par[:, 0:2, t], op=ALU.mult)
            shift = small.tile([P, 2], F32, tag="shift")
            nc.gpsimd.tensor_tensor(out=shift[:], in0=mean_var[:, :, 0], in1=slope[:], op=ALU.mult)
            nc.gpsimd.tensor_tensor(out=shift[:], in0=par[:, 2:4, t], in1=shift[:], op=ALU.subtract)
            slopes[n] = slope
            shifts[n] = shift

        def new_stats(n):
            stats_n = small.tile([P, 2, CHUNKS, STATS_DIM], F32, tag="stats")
            stats[n] = stats_n

        quantise_chunk(wx_words, wx_codes, wx_scales, 0)
        quantise_chunk(wh_words, wh_codes, wh_scales, 0)
        par_bank = psum.tile([P, P], BF16, tag="bank")
        nc.tensor.transpose(par_bank[:], par_rows[:], ident_bf16[:])
        par = const.tile([P, 4, GATE_TILES], F32)
        nc.vector.tensor_copy(out=par[:].rearrange("p q t -> p (q t)"), in_=par_bank[:, 0 : 4 * GATE_TILES])
        head_items = [divmod(i, CHUNKS) for i in range(LEAD)]
        for n, c in head_items:
            if c == 0:
                new_stats(n)
        activations = ((x_words, x_codes, x_scales), (h_words, h_codes, h_scales))
        head_chunks = [(s, chunk) for s in range(2) for chunk in range(CHUNKS)]
        for k in range(len(head_chunks) + HEAD_LAG):
            if k < len(head_chunks):
                s, chunk = head_chunks[k]
                quantise_chunk(*activations[s], chunk)
            if k >= HEAD_LAG:
                s, chunk = head_chunks[k - HEAD_LAG]
                for n, c in head_items:
                    if c == chunk:
                        chunk_statistics(s, n, c)
        for n, c in head_items:
            if c == CHUNKS - 1:
                coefficients(n)

        cell_t = keep.tile([P, HIDDEN_TILES, BATCH], BF16)
        half_tiles = ROW_TILES // 2
        next_grouped = {}

        def first_sweep(i):
            if i >= ITEMS:
                return
            n, c = divmod(i, CHUNKS)
            if c == 0:
                new_stats(n)
            for s in range(2):
                chunk_statistics(s, n, c)
            if c == CHUNKS - 1:
                coefficients(n)

        def norm_h(i):
            if i >= ITEMS:
                return
            n, c = divmod(i, CHUNKS)
            if c == 0:
                value = gates.tile([P, BATCH], F32, tag="gate")
                values[n] = value
            zh = project(1, n, c)
            nc.scalar.activation(
                out=values[n][:, chunk_cols(c)],
                in_=zh[:],
                func=ACT.Identity,
                scale=slopes[n][:, 1:2],
                bias=shifts[n][:, 1:2],
            )

        def norm_x(i):
            if i < 0 or i >= ITEMS:
                return
            n, c = divmod(i, CHUNKS)
            part = values[n][:, chunk_cols(c)]
            zx = project(0, n, c)
            nc.vector.scalar_tensor_tensor(
                out=part, in0=zx[:], scalar=slopes[n][:, 0:1], in1=part, op0=ALU.mult, op1=ALU.add
            )

        def gate_function(i):
            if i < 0 or i >= ITEMS:
                return
            n, c = divmod(i, CHUNKS)
            part = values[n][:, chunk_cols(c)]
            func = ACT.Tanh if order[n][1] == G_GATE else ACT.Sigmoid
            nc.scalar.activation(out=part, in_=part, func=func, bias=shifts[n][:, 0:1])

        def vector_is_free(n):
            return n + VECTOR_TILES >= GATE_TILES

        def due(i, lag, short_lag):
            items = []
            for item, on_vector in ((i - lag, False), (i - short_lag, True)):
                if 0 <= item < ITEMS and vector_is_free(item // CHUNKS) == on_vector:
                    items.append(item)
            return items

        def products_engine(n):
            return nc.vector if vector_is_free(n) else nc.gpsimd

        def first_product(i):
            n, c = divmod(i, CHUNKS)
            j, gate = order[n]
            cols = chunk_cols(c)
            mine = values[n][:, cols]
            candidate = values[j * GATES][:, cols]
            if gate == I_GATE:
                products_engine(n).tensor_tensor(out=candidate, in0=mine, in1=candidate, op=ALU.mult)
            if gate == F_GATE:
                products_engine(n).tensor_tensor(out=mine, in0=mine, in1=cell_t[:, j, cols], op=ALU.mult)

        def second_product(i):
            n, c = divmod(i, CHUNKS)
            j, gate = order[n]
            cols = chunk_cols(c)
            mine = values[n][:, cols]
            candidate = values[j * GATES][:, cols]
            if gate == F_GATE:
                products_engine(n).tensor_tensor(out=mine, in0=mine, in1=candidate, op=ALU.add)
            if gate == O_GATE:
                products_engine(n).tensor_tensor(out=mine, in0=mine, in1=candidate, op=ALU.mult)

        def cell_tanh(i):
            n, c = divmod(i, CHUNKS)
            j, gate = order[n]
            if gate == F_GATE:
                nc.scalar.activation(
                    out=values[j * GATES][:, chunk_cols(c)], in_=values[n][:, chunk_cols(c)], func=ACT.Tanh
                )

        def store(i):
            n, c = divmod(i, CHUNKS)
            j, gate = order[n]
            if gate != F_GATE and gate != O_GATE:
                return
            out = out_1 if gate == F_GATE else out_0
            bank = psum.tile([P, TILES_PER_CHUNK, P], F32, tag="bank")
            for t in range(TILES_PER_CHUNK):
                first = (c * TILES_PER_CHUNK + t) * P
                nc.tensor.transpose(bank[:, t, :], values[n][:, first : first + P], ident_f32[:])
            rows = rows_pool.tile([P, TILES_PER_CHUNK, P], F32, tag="rows")
            if vector_is_free(n):
                nc.vector.tensor_copy(out=rows[:], in_=bank[:])
            else:
                nc.scalar.copy(out=rows[:], in_=bank[:])
            out_rows = out.rearrange("(p t) k -> p t k", t=ROW_TILES)
            nc.sync.dma_start(out=out_rows[:, chunk_tiles(c), j * P : (j + 1) * P], in_=rows[:])

        def prepare(i):
            if i >= ITEMS:
                return
            n, c = divmod(i, CHUNKS)
            j, gate = order[n]
            if gate == G_GATE and j + 1 < HIDDEN_TILES:
                s, a = divmod(c, 2)
                if a == 0:
                    next_grouped[s] = new_grouped()
                transpose_256_rows((wx_words, wh_words)[s], j + 1, a, next_grouped[s])
            if gate == I_GATE and c == 0 and j + 1 < HIDDEN_TILES:
                quantise(next_grouped[0], wx_codes, wx_scales, j + 1)
                quantise(next_grouped[1], wh_codes, wh_scales, j + 1)
            if j == 0 and (gate == I_GATE or gate == F_GATE):
                jc, a = divmod(i - CHUNKS, 2)
                bank = psum.tile([P, half_tiles, P], BF16, tag="bank")
                for t in range(half_tiles):
                    nc.tensor.transpose(bank[:, t, :], c_sb[:, a * half_tiles + t, jc * P : (jc + 1) * P], ident_bf16[:])
                nc.scalar.copy(
                    out=cell_t[:, jc, a * half_tiles * P : (a + 1) * half_tiles * P],
                    in_=bank[:].rearrange("p t r -> p (t r)"),
                )

        for i in range(ITEMS + LAG_STORE):
            if i % 2 == 1:
                for item in due(i, LAG_STORE, SHORT_STORE):
                    store(item)
                prepare(i)
            norm_x(i - LAG_NORM_X)
            first_sweep(i + LEAD)
            norm_h(i)
            gate_function(i - LAG_FUNCTION)
            for item in due(i, LAG_FIRST_PRODUCT, SHORT_FIRST_PRODUCT):
                first_product(item)
            for item in due(i, LAG_SECOND_PRODUCT, SHORT_SECOND_PRODUCT):
                second_product(item)
            for item in due(i, LAG_TANH, SHORT_TANH):
                cell_tanh(item)
            if i % 2 == 0:
                for item in due(i, LAG_STORE, SHORT_STORE):
                    store(item)
                prepare(i)
